import numpy as np
import ml_dtypes

BF16 = ml_dtypes.bfloat16


def bf(x):
    return np.asarray(x, np.float32).astype(BF16)


def f32(x):
    return np.asarray(x, np.float32)


def f64(x):
    return np.asarray(x).astype(np.float64)


def striped(idx):
    return np.tile(idx.reshape(-1, 16).T, (8, 1))


C, S, N = 256, 256, 128


def logit(v, w1, b1, w2):
    return f64(w2).T @ np.tanh(f64(w1).T @ f64(v) + f64(b1))


def setup_inputs():
    return {
        "base": f32(np.random.standard_normal((C, S))),
        "title": f32(np.random.standard_normal((C, N))),
        "body": f32(np.random.standard_normal((C, N))),
        "cat": f32(np.random.standard_normal((C, N))),
        "w1": bf(np.random.standard_normal((C, C)) / np.sqrt(C)),
        "b1": f32(0.5 * np.random.standard_normal((C, 1))),
        "w2": bf(2.0 * np.random.standard_normal((C, 1)) / np.sqrt(C)),
        "offs": striped(np.random.permutation(S)[:N]),
    }


def reference(base, title, body, cat, w1, b1, w2, offs):
    idx = offs[:16].T.reshape(-1)
    xt = np.exp(logit(title, w1, b1, w2))
    xb = np.exp(logit(body, w1, b1, w2))
    xc = np.exp(logit(cat, w1, b1, w2))
    den = xt + xb + xc
    out = f64(base).copy()
    out[:, idx] = ((xt / den) * f64(title) + (xb / den) * f64(body)) + (xc / den) * f64(cat)
    return out

@@ -1,0 +1,89 @@
+import concourse.mybir as mybir
+
+P = 128
+C, S, N = 256, 256, 128
+CB = C // P
+VIEWS = 3
+F32, BF16, U16 = mybir.dt.float32, mybir.dt.bfloat16, mybir.dt.uint16
+ALU = mybir.AluOpType
+ACT = mybir.ActivationFunctionType
+X = mybir.AxisListType.X
+
+FLOPS = 2 * C * C * VIEWS * N + 2 * C * VIEWS * N
+
+
+def tile_naml_kernel(tc, base, title, body, cat, w1, b1, w2, offs, out):
+    nc = tc.nc
+    with tc.tile_pool(name="held", bufs=1) as held, tc.psum_pool(name="psum", bufs=1) as psum:
+        w1_sb = held.tile([P, CB, C], BF16, name="w1_sb")
+        nc.scalar.dma_start(w1_sb[:], w1.rearrange("(kb p) d -> p kb d", p=P))
+        view_sb = held.tile([P, CB, VIEWS, N], F32, name="view_sb")
+        for v, (view, queue) in enumerate(((title, nc.sync), (body, nc.scalar), (cat, nc.sync))):
+            queue.dma_start(view_sb[:, :, v, :], view.rearrange("(cb p) j -> p cb j", p=P))
+        b1_sb = held.tile([P, CB], F32, name="b1_sb")
+        w2_sb = held.tile([P, CB], BF16, name="w2_sb")
+        with nc.allow_non_contiguous_dma(reason="one element to a partition: 256 small pieces, once"):
+            nc.gpsimd.dma_start(b1_sb[:], b1.rearrange("(db p) o -> p (db o)", p=P))
+            nc.gpsimd.dma_start(w2_sb[:], w2.rearrange("(db p) o -> p (db o)", p=P))
+        offsets = held.tile([P, N // 16], U16, name="offsets")
+        nc.sync.dma_start(offsets[:], offs)
+        windows = []
+        for cb, queue in enumerate((nc.sync, nc.scalar)):
+            window = held.tile([P, S], F32, name=f"window{cb}")
+            queue.dma_start(window[:], base[cb * P : (cb + 1) * P, :])
+            windows.append(window)
+
+        w2_rep = held.tile([P, CB, P], BF16, name="w2_rep")
+        nc.vector.tensor_copy(w2_rep[:], w2_sb[:].unsqueeze(2).to_broadcast([P, CB, P]))
+
+        view_bf = held.tile([P, CB, VIEWS, N], BF16, name="view_bf")
+        for v in range(VIEWS):
+            nc.vector.tensor_copy(view_bf[:, :, v, :], view_sb[:, :, v, :])
+
+        hidden_bf = held.tile([P, CB, VIEWS * N], BF16, name="hidden_bf")
+        for db in range(CB):
+            hidden_ps = psum.tile([P, VIEWS * N], F32, name=f"hidden_ps{db}")
+            for kb in range(CB):
+                nc.tensor.matmul(
+                    hidden_ps[:],
+                    w1_sb[:, kb, db * P : (db + 1) * P],
+                    view_bf[:, kb, :, :],
+                    start=(kb == 0),
+                    stop=(kb == CB - 1),
+                )
+            nc.scalar.activation(hidden_bf[:, db, :], hidden_ps[:], ACT.Tanh, bias=b1_sb[:, db : db + 1])
+
+        logit_ps = psum.tile([P, VIEWS, N], F32, name="logit_ps")
+        for db in range(CB):
+            nc.tensor.matmul(
+                logit_ps[:], w2_rep[:, db, :], hidden_bf[:, db, :], start=(db == 0), stop=(db == CB - 1)
+            )
+
+        top = held.tile([P, N], F32, name="top")
+        nc.vector.tensor_reduce(top[:], logit_ps[:].rearrange("p v j -> p j v"), axis=X, op=ALU.max)
+        shifted = held.tile([P, VIEWS, N], F32, name="shifted")
+        nc.vector.tensor_tensor(
+            shifted[:], logit_ps[:], top[:].unsqueeze(1).to_broadcast([P, VIEWS, N]), ALU.subtract
+        )
+        grown = held.tile([P, VIEWS, N], F32, name="grown")
+        nc.scalar.activation(grown[:], shifted[:], ACT.Exp)
+        total = held.tile([P, N], F32, name="total")
+        nc.vector.tensor_reduce(total[:], grown[:].rearrange("p v j -> p j v"), axis=X, op=ALU.add)
+        inverse = held.tile([P, N], F32, name="inverse")
+        nc.vector.reciprocal(inverse[:], total[:])
+        weight = held.tile([P, VIEWS, N], F32, name="weight")
+        nc.vector.tensor_tensor(
+            weight[:], grown[:], inverse[:].unsqueeze(1).to_broadcast([P, VIEWS, N]), ALU.mult
+        )
+
+        scaled = held.tile([P, CB, VIEWS, N], F32, name="scaled")
+        nc.vector.tensor_tensor(
+            scaled[:], view_sb[:], weight[:].unsqueeze(1).to_broadcast([P, CB, VIEWS, N]), ALU.mult
+        )
+        first_two = held.tile([P, CB, N], F32, name="first_two")
+        nc.vector.tensor_tensor(first_two[:], scaled[:, :, 0, :], scaled[:, :, 1, :], ALU.add)
+        for cb, queue in enumerate((nc.sync, nc.scalar)):
+            nc.vector.tensor_tensor(
+                windows[cb][:].indirect(offsets[:]), first_two[:, cb, :], scaled[:, cb, 2, :], ALU.add
+            )
+            queue.dma_start(out[cb * P : (cb + 1) * P, :], windows[cb][:])

@@ -1,4 +1,5 @@
 import concourse.mybir as mybir
+from concourse.masks import make_identity
 
 P = 128
 C, S, N = 256, 256, 128
@@ -14,12 +15,18 @@ FLOPS = 2 * C * C * VIEWS * N + 2 * C * VIEWS * N
 
 def tile_naml_kernel(tc, base, title, body, cat, w1, b1, w2, offs, out):
     nc = tc.nc
-    with tc.tile_pool(name="held", bufs=1) as held, tc.psum_pool(name="psum", bufs=1) as psum:
+    with (
+        tc.tile_pool(name="held", bufs=1) as held,
+        tc.psum_pool(name="hidden_banks", bufs=2) as hidden_banks,
+        tc.psum_pool(name="psum", bufs=1) as psum,
+    ):
         w1_sb = held.tile([P, CB, C], BF16, name="w1_sb")
         nc.scalar.dma_start(w1_sb[:], w1.rearrange("(kb p) d -> p kb d", p=P))
-        view_sb = held.tile([P, CB, VIEWS, N], F32, name="view_sb")
+        view_sb = []
         for v, (view, queue) in enumerate(((title, nc.sync), (body, nc.scalar), (cat, nc.sync))):
-            queue.dma_start(view_sb[:, :, v, :], view.rearrange("(cb p) j -> p cb j", p=P))
+            loaded = held.tile([P, CB, N], F32, name=f"view_sb{v}")
+            queue.dma_start(loaded[:], view.rearrange("(cb p) j -> p cb j", p=P))
+            view_sb.append(loaded)
         b1_sb = held.tile([P, CB], F32, name="b1_sb")
         w2_sb = held.tile([P, CB], BF16, name="w2_sb")
         with nc.allow_non_contiguous_dma(reason="one element to a partition: 256 small pieces, once"):
@@ -32,58 +39,58 @@ def tile_naml_kernel(tc, base, title, body, cat, w1, b1, w2, offs, out):
             window = held.tile([P, S], F32, name=f"window{cb}")
             queue.dma_start(window[:], base[cb * P : (cb + 1) * P, :])
             windows.append(window)
+        identity = held.tile([P, P], F32, name="identity")
+        make_identity(nc, identity[:])
 
-        w2_rep = held.tile([P, CB, P], BF16, name="w2_rep")
-        nc.vector.tensor_copy(w2_rep[:], w2_sb[:].unsqueeze(2).to_broadcast([P, CB, P]))
-
-        view_bf = held.tile([P, CB, VIEWS, N], BF16, name="view_bf")
+        logit_ps = psum.tile([P, VIEWS], F32, name="logit_ps")
         for v in range(VIEWS):
-            nc.vector.tensor_copy(view_bf[:, :, v, :], view_sb[:, :, v, :])
-
-        hidden_bf = held.tile([P, CB, VIEWS * N], BF16, name="hidden_bf")
-        for db in range(CB):
-            hidden_ps = psum.tile([P, VIEWS * N], F32, name=f"hidden_ps{db}")
-            for kb in range(CB):
+            view_bf = held.tile([P, CB, N], BF16, name=f"view_bf{v}")
+            nc.vector.tensor_copy(view_bf[:], view_sb[v][:])
+            hidden_bf = held.tile([P, CB, N], BF16, name=f"hidden_bf{v}")
+            for db in range(CB):
+                hidden_ps = hidden_banks.tile([P, N], F32, name=f"hidden_ps{db}")
+                for kb in range(CB):
+                    nc.tensor.matmul(
+                        hidden_ps[:],
+                        w1_sb[:, kb, db * P : (db + 1) * P],
+                        view_bf[:, kb, :],
+                        start=(kb == 0),
+                        stop=(kb == CB - 1),
+                    )
+                nc.scalar.activation(hidden_bf[:, db, :], hidden_ps[:], ACT.Tanh, bias=b1_sb[:, db : db + 1])
+            for db in range(CB):
                 nc.tensor.matmul(
-                    hidden_ps[:],
-                    w1_sb[:, kb, db * P : (db + 1) * P],
-                    view_bf[:, kb, :, :],
-                    start=(kb == 0),
-                    stop=(kb == CB - 1),
+                    logit_ps[:, v : v + 1],
+                    hidden_bf[:, db, :],
+                    w2_sb[:, db : db + 1],
+                    start=(db == 0),
+                    stop=(db == CB - 1),
                 )
-            nc.scalar.activation(hidden_bf[:, db, :], hidden_ps[:], ACT.Tanh, bias=b1_sb[:, db : db + 1])
 
-        logit_ps = psum.tile([P, VIEWS, N], F32, name="logit_ps")
-        for db in range(CB):
-            nc.tensor.matmul(
-                logit_ps[:], w2_rep[:, db, :], hidden_bf[:, db, :], start=(db == 0), stop=(db == CB - 1)
-            )
-
-        top = held.tile([P, N], F32, name="top")
-        nc.vector.tensor_reduce(top[:], logit_ps[:].rearrange("p v j -> p j v"), axis=X, op=ALU.max)
-        shifted = held.tile([P, VIEWS, N], F32, name="shifted")
-        nc.vector.tensor_tensor(
-            shifted[:], logit_ps[:], top[:].unsqueeze(1).to_broadcast([P, VIEWS, N]), ALU.subtract
-        )
-        grown = held.tile([P, VIEWS, N], F32, name="grown")
-        nc.scalar.activation(grown[:], shifted[:], ACT.Exp)
-        total = held.tile([P, N], F32, name="total")
-        nc.vector.tensor_reduce(total[:], grown[:].rearrange("p v j -> p j v"), axis=X, op=ALU.add)
-        inverse = held.tile([P, N], F32, name="inverse")
+        minus_top = held.tile([P, 1], F32, name="minus_top")
+        nc.vector.tensor_reduce(minus_top[:], logit_ps[:], axis=X, op=ALU.max, negate=True)
+        grown = held.tile([P, VIEWS], F32, name="grown")
+        total = held.tile([P, 1], F32, name="total")
+        nc.scalar.activation(grown[:], logit_ps[:], ACT.Exp, bias=minus_top[:], accum_out=total[:])
+        inverse = held.tile([P, 1], F32, name="inverse")
         nc.vector.reciprocal(inverse[:], total[:])
-        weight = held.tile([P, VIEWS, N], F32, name="weight")
-        nc.vector.tensor_tensor(
-            weight[:], grown[:], inverse[:].unsqueeze(1).to_broadcast([P, VIEWS, N]), ALU.mult
-        )
+        weight = held.tile([P, VIEWS], F32, name="weight")
+        nc.vector.tensor_scalar_mul(weight[:], grown[:], inverse[:])
 
-        scaled = held.tile([P, CB, VIEWS, N], F32, name="scaled")
-        nc.vector.tensor_tensor(
-            scaled[:], view_sb[:], weight[:].unsqueeze(1).to_broadcast([P, CB, VIEWS, N]), ALU.mult
-        )
+        scaled = []
+        for v in range(VIEWS):
+            spread_ps = psum.tile([P, N], F32, name=f"spread_ps{v}")
+            nc.tensor.transpose(spread_ps[:], weight[:, v : v + 1].to_broadcast([N, P]), identity[:])
+            product = held.tile([P, CB, N], F32, name=f"scaled{v}")
+            nc.vector.tensor_tensor(
+                product[:], view_sb[v][:], spread_ps[:].unsqueeze(1).to_broadcast([P, CB, N]), ALU.mult
+            )
+            scaled.append(product)
+
         first_two = held.tile([P, CB, N], F32, name="first_two")
-        nc.vector.tensor_tensor(first_two[:], scaled[:, :, 0, :], scaled[:, :, 1, :], ALU.add)
+        nc.vector.tensor_tensor(first_two[:], scaled[0][:], scaled[1][:], ALU.add)
         for cb, queue in enumerate((nc.sync, nc.scalar)):
             nc.vector.tensor_tensor(
-                windows[cb][:].indirect(offsets[:]), first_two[:, cb, :], scaled[:, cb, 2, :], ALU.add
+                windows[cb][:].indirect(offsets[:]), first_two[:, cb, :], scaled[2][:, cb, :], ALU.add
             )
             queue.dma_start(out[cb * P : (cb + 1) * P, :], windows[cb][:])

@@ -17,38 +17,39 @@ def tile_naml_kernel(tc, base, title, body, cat, w1, b1, w2, offs, out):
     nc = tc.nc
     with (
         tc.tile_pool(name="held", bufs=1) as held,
-        tc.psum_pool(name="hidden_banks", bufs=2) as hidden_banks,
+        tc.psum_pool(name="hidden_banks", bufs=3) as hidden_banks,
         tc.psum_pool(name="psum", bufs=1) as psum,
     ):
-        w1_sb = held.tile([P, CB, C], BF16, name="w1_sb")
-        nc.scalar.dma_start(w1_sb[:], w1.rearrange("(kb p) d -> p kb d", p=P))
-        view_sb = []
-        for v, (view, queue) in enumerate(((title, nc.sync), (body, nc.scalar), (cat, nc.sync))):
-            loaded = held.tile([P, CB, N], F32, name=f"view_sb{v}")
-            queue.dma_start(loaded[:], view.rearrange("(cb p) j -> p cb j", p=P))
-            view_sb.append(loaded)
         b1_sb = held.tile([P, CB], F32, name="b1_sb")
         w2_sb = held.tile([P, CB], BF16, name="w2_sb")
-        with nc.allow_non_contiguous_dma(reason="one element to a partition: 256 small pieces, once"):
-            nc.gpsimd.dma_start(b1_sb[:], b1.rearrange("(db p) o -> p (db o)", p=P))
-            nc.gpsimd.dma_start(w2_sb[:], w2.rearrange("(db p) o -> p (db o)", p=P))
+        w1_sb = held.tile([P, CB, C], BF16, name="w1_sb")
+        view_sb = [held.tile([P, CB, N], F32, name=f"view_sb{v}") for v in range(VIEWS)]
         offsets = held.tile([P, N // 16], U16, name="offsets")
+        nc.scalar.dma_start(w1_sb[:], w1.rearrange("(kb p) d -> p kb d", p=P))
+        for v, (view, queue) in enumerate(((title, nc.sync), (body, nc.scalar), (cat, nc.sync))):
+            queue.dma_start(view_sb[v][:], view.rearrange("(cb p) j -> p cb j", p=P))
+        with nc.allow_non_contiguous_dma(reason="one element to a partition: 256 small pieces, once"):
+            nc.sync.dma_start(b1_sb[:], b1.rearrange("(db p) o -> p (db o)", p=P))
+            nc.scalar.dma_start(w2_sb[:], w2.rearrange("(db p) o -> p (db o)", p=P))
         nc.sync.dma_start(offsets[:], offs)
-        windows = []
-        for cb, queue in enumerate((nc.sync, nc.scalar)):
-            window = held.tile([P, S], F32, name=f"window{cb}")
-            queue.dma_start(window[:], base[cb * P : (cb + 1) * P, :])
-            windows.append(window)
+
+        scratch = held.tile([P, 1], F32, name="scratch")
+        nc.vector.memset(scratch[:], 0.0)
+        nc.scalar.activation(scratch[:], scratch[:], ACT.Tanh)
         identity = held.tile([P, P], F32, name="identity")
         make_identity(nc, identity[:])
+        windows = []
+        for cb in range(CB):
+            window = held.tile([P, S], F32, name=f"window{cb}")
+            nc.gpsimd.dma_start(window[:], base[cb * P : (cb + 1) * P, :])
+            windows.append(window)
 
-        logit_ps = psum.tile([P, VIEWS], F32, name="logit_ps")
+        hidden_bf = [held.tile([P, CB, N], BF16, name=f"hidden_bf{v}") for v in range(VIEWS)]
         for v in range(VIEWS):
             view_bf = held.tile([P, CB, N], BF16, name=f"view_bf{v}")
             nc.vector.tensor_copy(view_bf[:], view_sb[v][:])
-            hidden_bf = held.tile([P, CB, N], BF16, name=f"hidden_bf{v}")
             for db in range(CB):
-                hidden_ps = hidden_banks.tile([P, N], F32, name=f"hidden_ps{db}")
+                hidden_ps = hidden_banks.tile([P, N], F32, name="hidden_ps")
                 for kb in range(CB):
                     nc.tensor.matmul(
                         hidden_ps[:],
@@ -57,11 +58,14 @@ def tile_naml_kernel(tc, base, title, body, cat, w1, b1, w2, offs, out):
                         start=(kb == 0),
                         stop=(kb == CB - 1),
                     )
-                nc.scalar.activation(hidden_bf[:, db, :], hidden_ps[:], ACT.Tanh, bias=b1_sb[:, db : db + 1])
+                nc.scalar.activation(hidden_bf[v][:, db, :], hidden_ps[:], ACT.Tanh, bias=b1_sb[:, db : db + 1])
+
+        logit_ps = psum.tile([P, VIEWS], F32, name="logit_ps")
+        for v in range(VIEWS):
             for db in range(CB):
                 nc.tensor.matmul(
                     logit_ps[:, v : v + 1],
-                    hidden_bf[:, db, :],
+                    hidden_bf[v][:, db, :],
                     w2_sb[:, db : db + 1],
                     start=(db == 0),
                     stop=(db == CB - 1),

@@ -10,6 +10,9 @@ ALU = mybir.AluOpType
 ACT = mybir.ActivationFunctionType
 X = mybir.AxisListType.X
 
+WARM_COLUMNS = 512
+WARM_TURNS = 4
+
 FLOPS = 2 * C * C * VIEWS * N + 2 * C * VIEWS * N
 
 
@@ -32,6 +35,14 @@ def tile_naml_kernel(tc, base, title, body, cat, w1, b1, w2, offs, out):
             nc.sync.dma_start(b1_sb[:], b1.rearrange("(db p) o -> p (db o)", p=P))
             nc.scalar.dma_start(w2_sb[:], w2.rearrange("(db p) o -> p (db o)", p=P))
         nc.sync.dma_start(offsets[:], offs)
+
+        zero = held.tile([P, 1], BF16, name="zero")
+        nc.gpsimd.memset(zero[:], 0.0)
+        warm_ps = psum.tile([P, WARM_COLUMNS], F32, name="warm_ps")
+        for turn in range(WARM_TURNS):
+            nc.tensor.matmul(
+                warm_ps[:], zero[:].to_broadcast([P, P]), zero[:].to_broadcast([P, WARM_COLUMNS]), start=True, stop=True
+            )
 
         scratch = held.tile([P, 1], F32, name="scratch")
         nc.vector.memset(scratch[:], 0.0)

@@ -18,11 +18,7 @@ FLOPS = 2 * C * C * VIEWS * N + 2 * C * VIEWS * N
 
 def tile_naml_kernel(tc, base, title, body, cat, w1, b1, w2, offs, out):
     nc = tc.nc
-    with (
-        tc.tile_pool(name="held", bufs=1) as held,
-        tc.psum_pool(name="hidden_banks", bufs=3) as hidden_banks,
-        tc.psum_pool(name="psum", bufs=1) as psum,
-    ):
+    with tc.tile_pool(name="held", bufs=1) as held:
         b1_sb = held.tile([P, CB], F32, name="b1_sb")
         w2_sb = held.tile([P, CB], BF16, name="w2_sb")
         w1_sb = held.tile([P, CB, C], BF16, name="w1_sb")
@@ -38,11 +34,12 @@ def tile_naml_kernel(tc, base, title, body, cat, w1, b1, w2, offs, out):
 
         zero = held.tile([P, 1], BF16, name="zero")
         nc.gpsimd.memset(zero[:], 0.0)
-        warm_ps = psum.tile([P, WARM_COLUMNS], F32, name="warm_ps")
-        for turn in range(WARM_TURNS):
-            nc.tensor.matmul(
-                warm_ps[:], zero[:].to_broadcast([P, P]), zero[:].to_broadcast([P, WARM_COLUMNS]), start=True, stop=True
-            )
+        with tc.psum_pool(name="warm_bank", bufs=1) as warm_bank:
+            warm_ps = warm_bank.tile([P, WARM_COLUMNS], F32, name="warm_ps")
+            for turn in range(WARM_TURNS):
+                nc.tensor.matmul(
+                    warm_ps[:], zero[:].to_broadcast([P, P]), zero[:].to_broadcast([P, WARM_COLUMNS]), start=True, stop=True
+                )
 
         scratch = held.tile([P, 1], F32, name="scratch")
         nc.vector.memset(scratch[:], 0.0)
@@ -55,57 +52,62 @@ def tile_naml_kernel(tc, base, title, body, cat, w1, b1, w2, offs, out):
             nc.gpsimd.dma_start(window[:], base[cb * P : (cb + 1) * P, :])
             windows.append(window)
 
-        hidden_bf = [held.tile([P, CB, N], BF16, name=f"hidden_bf{v}") for v in range(VIEWS)]
-        for v in range(VIEWS):
-            view_bf = held.tile([P, CB, N], BF16, name=f"view_bf{v}")
-            nc.vector.tensor_copy(view_bf[:], view_sb[v][:])
-            for db in range(CB):
-                hidden_ps = hidden_banks.tile([P, N], F32, name="hidden_ps")
+        with (
+            tc.psum_pool(name="hidden_banks", bufs=2) as hidden_banks,
+            tc.psum_pool(name="psum", bufs=1) as psum,
+        ):
+            hidden_bf = [held.tile([P, CB, N], BF16, name=f"hidden_bf{v}") for v in range(VIEWS)]
+            for v in range(VIEWS):
+                view_bf = held.tile([P, CB, N], BF16, name=f"view_bf{v}")
+                hidden_ps = [hidden_banks.tile([P, N], F32, name=f"hidden_ps{db}") for db in range(CB)]
                 for kb in range(CB):
+                    nc.vector.tensor_copy(view_bf[:, kb, :], view_sb[v][:, kb, :])
+                    for db in range(CB):
+                        nc.tensor.matmul(
+                            hidden_ps[db][:],
+                            w1_sb[:, kb, db * P : (db + 1) * P],
+                            view_bf[:, kb, :],
+                            start=(kb == 0),
+                            stop=(kb == CB - 1),
+                        )
+                for db in range(CB):
+                    nc.scalar.activation(hidden_bf[v][:, db, :], hidden_ps[db][:], ACT.Tanh, bias=b1_sb[:, db : db + 1])
+
+            logit_ps = psum.tile([P, VIEWS], F32, name="logit_ps")
+            for v in range(VIEWS):
+                for db in range(CB):
                     nc.tensor.matmul(
-                        hidden_ps[:],
-                        w1_sb[:, kb, db * P : (db + 1) * P],
-                        view_bf[:, kb, :],
-                        start=(kb == 0),
-                        stop=(kb == CB - 1),
+                        logit_ps[:, v : v + 1],
+                        hidden_bf[v][:, db, :],
+                        w2_sb[:, db : db + 1],
+                        start=(db == 0),
+                        stop=(db == CB - 1),
                     )
-                nc.scalar.activation(hidden_bf[v][:, db, :], hidden_ps[:], ACT.Tanh, bias=b1_sb[:, db : db + 1])
 
-        logit_ps = psum.tile([P, VIEWS], F32, name="logit_ps")
-        for v in range(VIEWS):
-            for db in range(CB):
-                nc.tensor.matmul(
-                    logit_ps[:, v : v + 1],
-                    hidden_bf[v][:, db, :],
-                    w2_sb[:, db : db + 1],
-                    start=(db == 0),
-                    stop=(db == CB - 1),
+            minus_top = held.tile([P, 1], F32, name="minus_top")
+            nc.vector.tensor_reduce(minus_top[:], logit_ps[:], axis=X, op=ALU.max, negate=True)
+            grown = held.tile([P, VIEWS], F32, name="grown")
+            total = held.tile([P, 1], F32, name="total")
+            nc.scalar.activation(grown[:], logit_ps[:], ACT.Exp, bias=minus_top[:], accum_out=total[:])
+            inverse = held.tile([P, 1], F32, name="inverse")
+            nc.vector.reciprocal(inverse[:], total[:])
+            weight = held.tile([P, VIEWS], F32, name="weight")
+            nc.vector.tensor_scalar_mul(weight[:], grown[:], inverse[:])
+
+            scaled = []
+            for v in range(VIEWS):
+                spread_ps = psum.tile([P, N], F32, name=f"spread_ps{v}")
+                nc.tensor.transpose(spread_ps[:], weight[:, v : v + 1].to_broadcast([N, P]), identity[:])
+                product = held.tile([P, CB, N], F32, name=f"scaled{v}")
+                nc.vector.tensor_tensor(
+                    product[:], view_sb[v][:], spread_ps[:].unsqueeze(1).to_broadcast([P, CB, N]), ALU.mult
                 )
+                scaled.append(product)
 
-        minus_top = held.tile([P, 1], F32, name="minus_top")
-        nc.vector.tensor_reduce(minus_top[:], logit_ps[:], axis=X, op=ALU.max, negate=True)
-        grown = held.tile([P, VIEWS], F32, name="grown")
-        total = held.tile([P, 1], F32, name="total")
-        nc.scalar.activation(grown[:], logit_ps[:], ACT.Exp, bias=minus_top[:], accum_out=total[:])
-        inverse = held.tile([P, 1], F32, name="inverse")
-        nc.vector.reciprocal(inverse[:], total[:])
-        weight = held.tile([P, VIEWS], F32, name="weight")
-        nc.vector.tensor_scalar_mul(weight[:], grown[:], inverse[:])
-
-        scaled = []
-        for v in range(VIEWS):
-            spread_ps = psum.tile([P, N], F32, name=f"spread_ps{v}")
-            nc.tensor.transpose(spread_ps[:], weight[:, v : v + 1].to_broadcast([N, P]), identity[:])
-            product = held.tile([P, CB, N], F32, name=f"scaled{v}")
-            nc.vector.tensor_tensor(
-                product[:], view_sb[v][:], spread_ps[:].unsqueeze(1).to_broadcast([P, CB, N]), ALU.mult
-            )
-            scaled.append(product)
-
-        first_two = held.tile([P, CB, N], F32, name="first_two")
-        nc.vector.tensor_tensor(first_two[:], scaled[0][:], scaled[1][:], ALU.add)
-        for cb, queue in enumerate((nc.sync, nc.scalar)):
-            nc.vector.tensor_tensor(
-                windows[cb][:].indirect(offsets[:]), first_two[:, cb, :], scaled[2][:, cb, :], ALU.add
-            )
-            queue.dma_start(out[cb * P : (cb + 1) * P, :], windows[cb][:])
+            first_two = held.tile([P, CB, N], F32, name="first_two")
+            nc.vector.tensor_tensor(first_two[:], scaled[0][:], scaled[1][:], ALU.add)
+            for cb, queue in enumerate((nc.sync, nc.scalar)):
+                nc.vector.tensor_tensor(
+                    windows[cb][:].indirect(offsets[:]), first_two[:, cb, :], scaled[2][:, cb, :], ALU.add
+                )
+                queue.dma_start(out[cb * P : (cb + 1) * P, :], windows[cb][:])

@@ -11,7 +11,7 @@ ACT = mybir.ActivationFunctionType
 X = mybir.AxisListType.X
 
 WARM_COLUMNS = 512
-WARM_TURNS = 4
+WARM_TURNS = 6
 
 FLOPS = 2 * C * C * VIEWS * N + 2 * C * VIEWS * N
 

@@ -11,7 +11,7 @@ ACT = mybir.ActivationFunctionType
 X = mybir.AxisListType.X
 
 WARM_COLUMNS = 512
-WARM_TURNS = 6
+WARM_TURNS = 4
 
 FLOPS = 2 * C * C * VIEWS * N + 2 * C * VIEWS * N
 
@@ -31,6 +31,11 @@ def tile_naml_kernel(tc, base, title, body, cat, w1, b1, w2, offs, out):
             nc.sync.dma_start(b1_sb[:], b1.rearrange("(db p) o -> p (db o)", p=P))
             nc.scalar.dma_start(w2_sb[:], w2.rearrange("(db p) o -> p (db o)", p=P))
         nc.sync.dma_start(offsets[:], offs)
+        windows = []
+        for cb in range(CB):
+            window = held.tile([P, S], F32, name=f"window{cb}")
+            nc.sync.dma_start(window[:], base[cb * P : (cb + 1) * P, :])
+            windows.append(window)
 
         zero = held.tile([P, 1], BF16, name="zero")
         nc.gpsimd.memset(zero[:], 0.0)
@@ -46,11 +51,6 @@ def tile_naml_kernel(tc, base, title, body, cat, w1, b1, w2, offs, out):
         nc.scalar.activation(scratch[:], scratch[:], ACT.Tanh)
         identity = held.tile([P, P], F32, name="identity")
         make_identity(nc, identity[:])
-        windows = []
-        for cb in range(CB):
-            window = held.tile([P, S], F32, name=f"window{cb}")
-            nc.gpsimd.dma_start(window[:], base[cb * P : (cb + 1) * P, :])
-            windows.append(window)
 
         with (
             tc.psum_pool(name="hidden_banks", bufs=2) as hidden_banks,
@@ -94,18 +94,19 @@ def tile_naml_kernel(tc, base, title, body, cat, w1, b1, w2, offs, out):
             weight = held.tile([P, VIEWS], F32, name="weight")
             nc.vector.tensor_scalar_mul(weight[:], grown[:], inverse[:])
 
-            scaled = []
+            spread_ps = [psum.tile([P, N], F32, name=f"spread_ps{v}") for v in range(VIEWS)]
             for v in range(VIEWS):
-                spread_ps = psum.tile([P, N], F32, name=f"spread_ps{v}")
-                nc.tensor.transpose(spread_ps[:], weight[:, v : v + 1].to_broadcast([N, P]), identity[:])
-                product = held.tile([P, CB, N], F32, name=f"scaled{v}")
+                nc.tensor.transpose(spread_ps[v][:], weight[:, v : v + 1].to_broadcast([N, P]), identity[:])
+            scaled = [held.tile([P, CB, N], F32, name=f"scaled{v}") for v in range(VIEWS)]
+            for v in range(2):
                 nc.vector.tensor_tensor(
-                    product[:], view_sb[v][:], spread_ps[:].unsqueeze(1).to_broadcast([P, CB, N]), ALU.mult
+                    scaled[v][:], view_sb[v][:], spread_ps[v][:].unsqueeze(1).to_broadcast([P, CB, N]), ALU.mult
                 )
-                scaled.append(product)
-
             first_two = held.tile([P, CB, N], F32, name="first_two")
             nc.vector.tensor_tensor(first_two[:], scaled[0][:], scaled[1][:], ALU.add)
+            for cb in range(CB):
+                nc.vector.tensor_tensor(scaled[2][:, cb, :], view_sb[2][:, cb, :], spread_ps[2][:], ALU.mult)
+
             for cb, queue in enumerate((nc.sync, nc.scalar)):
                 nc.vector.tensor_tensor(
                     windows[cb][:].indirect(offsets[:]), first_two[:, cb, :], scaled[2][:, cb, :], ALU.add

@@ -52,37 +52,40 @@ def tile_naml_kernel(tc, base, title, body, cat, w1, b1, w2, offs, out):
         identity = held.tile([P, P], F32, name="identity")
         make_identity(nc, identity[:])
 
-        with (
-            tc.psum_pool(name="hidden_banks", bufs=2) as hidden_banks,
-            tc.psum_pool(name="psum", bufs=1) as psum,
-        ):
-            hidden_bf = [held.tile([P, CB, N], BF16, name=f"hidden_bf{v}") for v in range(VIEWS)]
-            for v in range(VIEWS):
-                view_bf = held.tile([P, CB, N], BF16, name=f"view_bf{v}")
-                hidden_ps = [hidden_banks.tile([P, N], F32, name=f"hidden_ps{db}") for db in range(CB)]
-                for kb in range(CB):
-                    nc.vector.tensor_copy(view_bf[:, kb, :], view_sb[v][:, kb, :])
+        hidden_bf = [held.tile([P, CB, N], BF16, name=f"hidden_bf{v}") for v in range(VIEWS)]
+        with tc.psum_pool(name="psum", bufs=1) as psum:
+            cat_turned_ps = psum.tile([P, C], F32, name="cat_turned_ps")
+            logit_ps = psum.tile([P, VIEWS], F32, name="logit_ps")
+
+            with tc.psum_pool(name="hidden_banks", bufs=2) as hidden_banks:
+                for v in range(VIEWS):
+                    view_bf = held.tile([P, CB, N], BF16, name=f"view_bf{v}")
+                    hidden_ps = [hidden_banks.tile([P, N], F32, name=f"hidden_ps{db}") for db in range(CB)]
+                    for kb in range(CB):
+                        nc.vector.tensor_copy(view_bf[:, kb, :], view_sb[v][:, kb, :])
+                        for db in range(CB):
+                            nc.tensor.matmul(
+                                hidden_ps[db][:],
+                                w1_sb[:, kb, db * P : (db + 1) * P],
+                                view_bf[:, kb, :],
+                                start=(kb == 0),
+                                stop=(kb == CB - 1),
+                            )
+                    for db in range(CB):
+                        nc.scalar.activation(hidden_bf[v][:, db, :], hidden_ps[db][:], ACT.Tanh, bias=b1_sb[:, db : db + 1])
+
+                for cb in range(CB):
+                    nc.tensor.transpose(cat_turned_ps[:, cb * P : (cb + 1) * P], view_sb[2][:, cb, :], identity[:])
+
+                for v in range(VIEWS):
                     for db in range(CB):
                         nc.tensor.matmul(
-                            hidden_ps[db][:],
-                            w1_sb[:, kb, db * P : (db + 1) * P],
-                            view_bf[:, kb, :],
-                            start=(kb == 0),
-                            stop=(kb == CB - 1),
+                            logit_ps[:, v : v + 1],
+                            hidden_bf[v][:, db, :],
+                            w2_sb[:, db : db + 1],
+                            start=(db == 0),
+                            stop=(db == CB - 1),
                         )
-                for db in range(CB):
-                    nc.scalar.activation(hidden_bf[v][:, db, :], hidden_ps[db][:], ACT.Tanh, bias=b1_sb[:, db : db + 1])
-
-            logit_ps = psum.tile([P, VIEWS], F32, name="logit_ps")
-            for v in range(VIEWS):
-                for db in range(CB):
-                    nc.tensor.matmul(
-                        logit_ps[:, v : v + 1],
-                        hidden_bf[v][:, db, :],
-                        w2_sb[:, db : db + 1],
-                        start=(db == 0),
-                        stop=(db == CB - 1),
-                    )
 
             minus_top = held.tile([P, 1], F32, name="minus_top")
             nc.vector.tensor_reduce(minus_top[:], logit_ps[:], axis=X, op=ALU.max, negate=True)
@@ -94,21 +97,40 @@ def tile_naml_kernel(tc, base, title, body, cat, w1, b1, w2, offs, out):
             weight = held.tile([P, VIEWS], F32, name="weight")
             nc.vector.tensor_scalar_mul(weight[:], grown[:], inverse[:])
 
-            spread_ps = [psum.tile([P, N], F32, name=f"spread_ps{v}") for v in range(VIEWS)]
-            for v in range(VIEWS):
-                nc.tensor.transpose(spread_ps[v][:], weight[:, v : v + 1].to_broadcast([N, P]), identity[:])
-            scaled = [held.tile([P, CB, N], F32, name=f"scaled{v}") for v in range(VIEWS)]
-            for v in range(2):
-                nc.vector.tensor_tensor(
-                    scaled[v][:], view_sb[v][:], spread_ps[v][:].unsqueeze(1).to_broadcast([P, CB, N]), ALU.mult
-                )
-            first_two = held.tile([P, CB, N], F32, name="first_two")
-            nc.vector.tensor_tensor(first_two[:], scaled[0][:], scaled[1][:], ALU.add)
-            for cb in range(CB):
-                nc.vector.tensor_tensor(scaled[2][:, cb, :], view_sb[2][:, cb, :], spread_ps[2][:], ALU.mult)
+            with tc.psum_pool(name="late_banks", bufs=1) as late_banks:
+                spread_ps = [late_banks.tile([P, N], F32, name=f"spread_ps{v}") for v in range(2)]
+                for v in range(2):
+                    nc.tensor.transpose(spread_ps[v][:], weight[:, v : v + 1].to_broadcast([N, P]), identity[:])
 
-            for cb, queue in enumerate((nc.sync, nc.scalar)):
-                nc.vector.tensor_tensor(
-                    windows[cb][:].indirect(offsets[:]), first_two[:, cb, :], scaled[2][:, cb, :], ALU.add
-                )
-                queue.dma_start(out[cb * P : (cb + 1) * P, :], windows[cb][:])
+                cat_scaled_turned = held.tile([P, C], F32, name="cat_scaled_turned")
+                cat_scaled = held.tile([P, CB, N], F32, name="cat_scaled")
+                scaled = [held.tile([P, CB, N], F32, name=f"scaled{v}") for v in range(2)]
+                first_two = held.tile([P, CB, N], F32, name="first_two")
+
+                def scale_cat(cb):
+                    block = slice(cb * P, (cb + 1) * P)
+                    nc.vector.tensor_scalar_mul(cat_scaled_turned[:, block], cat_turned_ps[:, block], weight[:, 2:3])
+                    cat_scaled_ps = late_banks.tile([P, N], F32, name=f"cat_scaled_ps{cb}")
+                    nc.tensor.transpose(cat_scaled_ps[:], cat_scaled_turned[:, block], identity[:])
+                    nc.scalar.copy(cat_scaled[:, cb, :], cat_scaled_ps[:])
+
+                def scale(v, cb):
+                    nc.vector.tensor_tensor(scaled[v][:, cb, :], view_sb[v][:, cb, :], spread_ps[v][:], ALU.mult)
+
+                def add_first_two(cb):
+                    nc.vector.tensor_tensor(first_two[:, cb, :], scaled[0][:, cb, :], scaled[1][:, cb, :], ALU.add)
+
+                scale_cat(0)
+                scale(0, 0)
+                scale(1, 0)
+                scale(0, 1)
+                scale(1, 1)
+                add_first_two(0)
+                scale_cat(1)
+                add_first_two(1)
+
+                for cb, queue in enumerate((nc.sync, nc.scalar)):
+                    nc.vector.tensor_tensor(
+                        windows[cb][:].indirect(offsets[:]), first_two[:, cb, :], cat_scaled[:, cb, :], ALU.add
+                    )
+                    queue.dma_start(out[cb * P : (cb + 1) * P, :], windows[cb][:])

@@ -54,7 +54,7 @@ def tile_naml_kernel(tc, base, title, body, cat, w1, b1, w2, offs, out):
 
         hidden_bf = [held.tile([P, CB, N], BF16, name=f"hidden_bf{v}") for v in range(VIEWS)]
         with tc.psum_pool(name="psum", bufs=1) as psum:
-            cat_turned_ps = psum.tile([P, C], F32, name="cat_turned_ps")
+            early_logit_ps = psum.tile([P, 2], F32, name="early_logit_ps")
             logit_ps = psum.tile([P, VIEWS], F32, name="logit_ps")
 
             with tc.psum_pool(name="hidden_banks", bufs=2) as hidden_banks:
@@ -74,63 +74,62 @@ def tile_naml_kernel(tc, base, title, body, cat, w1, b1, w2, offs, out):
                     for db in range(CB):
                         nc.scalar.activation(hidden_bf[v][:, db, :], hidden_ps[db][:], ACT.Tanh, bias=b1_sb[:, db : db + 1])
 
-                for cb in range(CB):
-                    nc.tensor.transpose(cat_turned_ps[:, cb * P : (cb + 1) * P], view_sb[2][:, cb, :], identity[:])
-
-                for v in range(VIEWS):
+                def second_matmul(logit_column, v):
                     for db in range(CB):
                         nc.tensor.matmul(
-                            logit_ps[:, v : v + 1],
-                            hidden_bf[v][:, db, :],
-                            w2_sb[:, db : db + 1],
-                            start=(db == 0),
-                            stop=(db == CB - 1),
+                            logit_column, hidden_bf[v][:, db, :], w2_sb[:, db : db + 1], start=(db == 0), stop=(db == CB - 1)
                         )
 
+                for v in range(2):
+                    second_matmul(early_logit_ps[:, v : v + 1], v)
+                for v in range(VIEWS):
+                    second_matmul(logit_ps[:, v : v + 1], v)
+
             minus_top = held.tile([P, 1], F32, name="minus_top")
-            nc.vector.tensor_reduce(minus_top[:], logit_ps[:], axis=X, op=ALU.max, negate=True)
-            grown = held.tile([P, VIEWS], F32, name="grown")
+            nc.vector.tensor_reduce(minus_top[:], early_logit_ps[:], axis=X, op=ALU.max, negate=True)
+            grown = held.tile([P, 2], F32, name="grown")
+            early_sum = held.tile([P, 1], F32, name="early_sum")
+            nc.scalar.activation(grown[:], early_logit_ps[:], ACT.Exp, bias=minus_top[:], accum_out=early_sum[:])
+            grown_again = held.tile([P, VIEWS], F32, name="grown_again")
             total = held.tile([P, 1], F32, name="total")
-            nc.scalar.activation(grown[:], logit_ps[:], ACT.Exp, bias=minus_top[:], accum_out=total[:])
-            inverse = held.tile([P, 1], F32, name="inverse")
-            nc.vector.reciprocal(inverse[:], total[:])
-            weight = held.tile([P, VIEWS], F32, name="weight")
-            nc.vector.tensor_scalar_mul(weight[:], grown[:], inverse[:])
+            nc.scalar.activation(grown_again[:], logit_ps[:], ACT.Exp, bias=minus_top[:], accum_out=total[:])
 
             with tc.psum_pool(name="late_banks", bufs=1) as late_banks:
-                spread_ps = [late_banks.tile([P, N], F32, name=f"spread_ps{v}") for v in range(2)]
-                for v in range(2):
-                    nc.tensor.transpose(spread_ps[v][:], weight[:, v : v + 1].to_broadcast([N, P]), identity[:])
+                def spread(column, name):
+                    spread_ps = late_banks.tile([P, N], F32, name=name)
+                    nc.tensor.transpose(spread_ps[:], column.to_broadcast([N, P]), identity[:])
+                    return spread_ps
 
-                cat_scaled_turned = held.tile([P, C], F32, name="cat_scaled_turned")
-                cat_scaled = held.tile([P, CB, N], F32, name="cat_scaled")
-                scaled = [held.tile([P, CB, N], F32, name=f"scaled{v}") for v in range(2)]
+                grown_spread_ps = [spread(grown[:, v : v + 1], f"grown_spread_ps{v}") for v in range(2)]
+
+                minus_early_sum = held.tile([P, 1], F32, name="minus_early_sum")
+                inverse = held.tile([P, 1], F32, name="inverse")
+                cat_weight = held.tile([P, 1], F32, name="cat_weight")
+                scaled = [held.tile([P, CB, N], F32, name=f"scaled{v}") for v in range(VIEWS)]
+                summed = held.tile([P, CB, N], F32, name="summed")
                 first_two = held.tile([P, CB, N], F32, name="first_two")
 
-                def scale_cat(cb):
-                    block = slice(cb * P, (cb + 1) * P)
-                    nc.vector.tensor_scalar_mul(cat_scaled_turned[:, block], cat_turned_ps[:, block], weight[:, 2:3])
-                    cat_scaled_ps = late_banks.tile([P, N], F32, name=f"cat_scaled_ps{cb}")
-                    nc.tensor.transpose(cat_scaled_ps[:], cat_scaled_turned[:, block], identity[:])
-                    nc.scalar.copy(cat_scaled[:, cb, :], cat_scaled_ps[:])
+                def scale(v, cb, spread_ps):
+                    nc.vector.tensor_tensor(scaled[v][:, cb, :], view_sb[v][:, cb, :], spread_ps[:], ALU.mult)
 
-                def scale(v, cb):
-                    nc.vector.tensor_tensor(scaled[v][:, cb, :], view_sb[v][:, cb, :], spread_ps[v][:], ALU.mult)
-
-                def add_first_two(cb):
-                    nc.vector.tensor_tensor(first_two[:, cb, :], scaled[0][:, cb, :], scaled[1][:, cb, :], ALU.add)
-
-                scale_cat(0)
-                scale(0, 0)
-                scale(1, 0)
-                scale(0, 1)
-                scale(1, 1)
-                add_first_two(0)
-                scale_cat(1)
-                add_first_two(1)
+                nc.vector.tensor_scalar_mul(minus_early_sum[:], early_sum[:], -1.0)
+                nc.vector.reciprocal(inverse[:], total[:])
+                inverse_spread_ps = spread(inverse[:], "inverse_spread_ps")
+                scale(0, 0, grown_spread_ps[0])
+                scale(1, 0, grown_spread_ps[1])
+                nc.vector.tensor_scalar(cat_weight[:], inverse[:], minus_early_sum[:], 1.0, ALU.mult, ALU.add)
+                cat_weight_spread_ps = spread(cat_weight[:], "cat_weight_spread_ps")
+                scale(0, 1, grown_spread_ps[0])
+                scale(1, 1, grown_spread_ps[1])
+                for cb in range(CB):
+                    nc.vector.tensor_tensor(summed[:, cb, :], scaled[0][:, cb, :], scaled[1][:, cb, :], ALU.add)
+                for cb in range(CB):
+                    nc.vector.tensor_tensor(first_two[:, cb, :], summed[:, cb, :], inverse_spread_ps[:], ALU.mult)
+                for cb in range(CB):
+                    scale(2, cb, cat_weight_spread_ps)
 
                 for cb, queue in enumerate((nc.sync, nc.scalar)):
                     nc.vector.tensor_tensor(
-                        windows[cb][:].indirect(offsets[:]), first_two[:, cb, :], cat_scaled[:, cb, :], ALU.add
+                        windows[cb][:].indirect(offsets[:]), first_two[:, cb, :], scaled[2][:, cb, :], ALU.add
                     )
                     queue.dma_start(out[cb * P : (cb + 1) * P, :], windows[cb][:])

@@ -24,17 +24,19 @@ def tile_naml_kernel(tc, base, title, body, cat, w1, b1, w2, offs, out):
         w1_sb = held.tile([P, CB, C], BF16, name="w1_sb")
         view_sb = [held.tile([P, CB, N], F32, name=f"view_sb{v}") for v in range(VIEWS)]
         offsets = held.tile([P, N // 16], U16, name="offsets")
-        nc.scalar.dma_start(w1_sb[:], w1.rearrange("(kb p) d -> p kb d", p=P))
+        nc.scalar.dma_start(w1_sb[:], w1.rearrange("(p kb) d -> p kb d", p=P))
         for v, (view, queue) in enumerate(((title, nc.sync), (body, nc.scalar), (cat, nc.sync))):
-            queue.dma_start(view_sb[v][:], view.rearrange("(cb p) j -> p cb j", p=P))
+            queue.dma_start(view_sb[v][:], view.rearrange("(p cb) j -> p cb j", p=P))
         with nc.allow_non_contiguous_dma(reason="one element to a partition: 256 small pieces, once"):
             nc.sync.dma_start(b1_sb[:], b1.rearrange("(db p) o -> p (db o)", p=P))
             nc.scalar.dma_start(w2_sb[:], w2.rearrange("(db p) o -> p (db o)", p=P))
         nc.sync.dma_start(offsets[:], offs)
+        base_blocks = base.rearrange("(p cb) s -> p cb s", p=P)
+        out_blocks = out.rearrange("(p cb) s -> p cb s", p=P)
         windows = []
         for cb in range(CB):
             window = held.tile([P, S], F32, name=f"window{cb}")
-            nc.sync.dma_start(window[:], base[cb * P : (cb + 1) * P, :])
+            nc.sync.dma_start(window[:], base_blocks[:, cb, :])
             windows.append(window)
 
         zero = held.tile([P, 1], BF16, name="zero")
@@ -132,4 +134,4 @@ def tile_naml_kernel(tc, base, title, body, cat, w1, b1, w2, offs, out):
                     nc.vector.tensor_tensor(
                         windows[cb][:].indirect(offsets[:]), first_two[:, cb, :], scaled[2][:, cb, :], ALU.add
                     )
-                    queue.dma_start(out[cb * P : (cb + 1) * P, :], windows[cb][:])
+                    queue.dma_start(out_blocks[:, cb, :], windows[cb][:])

@@ -5,10 +5,13 @@ P = 128
 C, S, N = 256, 256, 128
 CB = C // P
 VIEWS = 3
+TITLE, BODY, CAT = 0, 1, 2
 F32, BF16, U16 = mybir.dt.float32, mybir.dt.bfloat16, mybir.dt.uint16
 ALU = mybir.AluOpType
 ACT = mybir.ActivationFunctionType
-X = mybir.AxisListType.X
+
+SIGNS = ((1.0, 0.0, 0.0, 1.0), (0.0, 1.0, 0.0, -1.0), (-1.0, -1.0, 0.0, 0.0))
+DIFFERENCES = VIEWS + 1
 
 WARM_COLUMNS = 512
 WARM_TURNS = 4
@@ -55,83 +58,91 @@ def tile_naml_kernel(tc, base, title, body, cat, w1, b1, w2, offs, out):
         make_identity(nc, identity[:])
 
         hidden_bf = [held.tile([P, CB, N], BF16, name=f"hidden_bf{v}") for v in range(VIEWS)]
-        with tc.psum_pool(name="psum", bufs=1) as psum:
-            early_logit_ps = psum.tile([P, 2], F32, name="early_logit_ps")
-            logit_ps = psum.tile([P, VIEWS], F32, name="logit_ps")
+        with (
+            tc.psum_pool(name="small_banks", bufs=1) as small_banks,
+            tc.psum_pool(name="hidden_banks", bufs=2) as hidden_banks,
+        ):
+            title_over_body_ps = small_banks.tile([P, 1], F32, name="title_over_body_ps")
+            over_cat_ps = small_banks.tile([P, VIEWS], F32, name="over_cat_ps")
 
-            with tc.psum_pool(name="hidden_banks", bufs=2) as hidden_banks:
-                for v in range(VIEWS):
-                    view_bf = held.tile([P, CB, N], BF16, name=f"view_bf{v}")
-                    hidden_ps = [hidden_banks.tile([P, N], F32, name=f"hidden_ps{db}") for db in range(CB)]
-                    for kb in range(CB):
-                        nc.vector.tensor_copy(view_bf[:, kb, :], view_sb[v][:, kb, :])
-                        for db in range(CB):
-                            nc.tensor.matmul(
-                                hidden_ps[db][:],
-                                w1_sb[:, kb, db * P : (db + 1) * P],
-                                view_bf[:, kb, :],
-                                start=(kb == 0),
-                                stop=(kb == CB - 1),
-                            )
-                    for db in range(CB):
-                        nc.scalar.activation(hidden_bf[v][:, db, :], hidden_ps[db][:], ACT.Tanh, bias=b1_sb[:, db : db + 1])
-
-                def second_matmul(logit_column, v):
+            for v in range(VIEWS):
+                view_bf = held.tile([P, CB, N], BF16, name=f"view_bf{v}")
+                hidden_ps = [hidden_banks.tile([P, N], F32, name=f"hidden_ps{db}") for db in range(CB)]
+                for kb in range(CB):
+                    nc.vector.tensor_copy(view_bf[:, kb, :], view_sb[v][:, kb, :])
                     for db in range(CB):
                         nc.tensor.matmul(
-                            logit_column, hidden_bf[v][:, db, :], w2_sb[:, db : db + 1], start=(db == 0), stop=(db == CB - 1)
+                            hidden_ps[db][:],
+                            w1_sb[:, kb, db * P : (db + 1) * P],
+                            view_bf[:, kb, :],
+                            start=(kb == 0),
+                            stop=(kb == CB - 1),
                         )
+                for db in range(CB):
+                    nc.scalar.activation(hidden_bf[v][:, db, :], hidden_ps[db][:], ACT.Tanh, bias=b1_sb[:, db : db + 1])
 
-                for v in range(2):
-                    second_matmul(early_logit_ps[:, v : v + 1], v)
-                for v in range(VIEWS):
-                    second_matmul(logit_ps[:, v : v + 1], v)
+            w2_signed = held.tile([P, CB, VIEWS, DIFFERENCES], BF16, name="w2_signed")
+            nc.vector.memset(w2_signed[:], 0.0)
+            for v in range(VIEWS):
+                for difference in range(DIFFERENCES):
+                    if SIGNS[v][difference] != 0.0:
+                        nc.vector.tensor_scalar_mul(w2_signed[:, :, v, difference], w2_sb[:], SIGNS[v][difference])
 
-            minus_top = held.tile([P, 1], F32, name="minus_top")
-            nc.vector.tensor_reduce(minus_top[:], early_logit_ps[:], axis=X, op=ALU.max, negate=True)
-            grown = held.tile([P, 2], F32, name="grown")
-            early_sum = held.tile([P, 1], F32, name="early_sum")
-            nc.scalar.activation(grown[:], early_logit_ps[:], ACT.Exp, bias=minus_top[:], accum_out=early_sum[:])
-            grown_again = held.tile([P, VIEWS], F32, name="grown_again")
-            total = held.tile([P, 1], F32, name="total")
-            nc.scalar.activation(grown_again[:], logit_ps[:], ACT.Exp, bias=minus_top[:], accum_out=total[:])
+            both = held.tile([P, CB, N], F32, name="both")
+            apart = held.tile([P, CB, N], F32, name="apart")
+            nc.vector.tensor_tensor(both[:], view_sb[TITLE][:], view_sb[BODY][:], ALU.add)
+            nc.vector.tensor_tensor(apart[:], view_sb[TITLE][:], view_sb[BODY][:], ALU.subtract)
 
-            with tc.psum_pool(name="late_banks", bufs=1) as late_banks:
-                def spread(column, name):
-                    spread_ps = late_banks.tile([P, N], F32, name=name)
-                    nc.tensor.transpose(spread_ps[:], column.to_broadcast([N, P]), identity[:])
-                    return spread_ps
-
-                grown_spread_ps = [spread(grown[:, v : v + 1], f"grown_spread_ps{v}") for v in range(2)]
-
-                minus_early_sum = held.tile([P, 1], F32, name="minus_early_sum")
-                inverse = held.tile([P, 1], F32, name="inverse")
-                cat_weight = held.tile([P, 1], F32, name="cat_weight")
-                scaled = [held.tile([P, CB, N], F32, name=f"scaled{v}") for v in range(VIEWS)]
-                summed = held.tile([P, CB, N], F32, name="summed")
-                first_two = held.tile([P, CB, N], F32, name="first_two")
-
-                def scale(v, cb, spread_ps):
-                    nc.vector.tensor_tensor(scaled[v][:, cb, :], view_sb[v][:, cb, :], spread_ps[:], ALU.mult)
-
-                nc.vector.tensor_scalar_mul(minus_early_sum[:], early_sum[:], -1.0)
-                nc.vector.reciprocal(inverse[:], total[:])
-                inverse_spread_ps = spread(inverse[:], "inverse_spread_ps")
-                scale(0, 0, grown_spread_ps[0])
-                scale(1, 0, grown_spread_ps[1])
-                nc.vector.tensor_scalar(cat_weight[:], inverse[:], minus_early_sum[:], 1.0, ALU.mult, ALU.add)
-                cat_weight_spread_ps = spread(cat_weight[:], "cat_weight_spread_ps")
-                scale(0, 1, grown_spread_ps[0])
-                scale(1, 1, grown_spread_ps[1])
-                for cb in range(CB):
-                    nc.vector.tensor_tensor(summed[:, cb, :], scaled[0][:, cb, :], scaled[1][:, cb, :], ALU.add)
-                for cb in range(CB):
-                    nc.vector.tensor_tensor(first_two[:, cb, :], summed[:, cb, :], inverse_spread_ps[:], ALU.mult)
-                for cb in range(CB):
-                    scale(2, cb, cat_weight_spread_ps)
-
-                for cb, queue in enumerate((nc.sync, nc.scalar)):
-                    nc.vector.tensor_tensor(
-                        windows[cb][:].indirect(offsets[:]), first_two[:, cb, :], scaled[2][:, cb, :], ALU.add
+            for v in range(VIEWS):
+                for db in range(CB):
+                    if v != CAT:
+                        nc.tensor.matmul(
+                            title_over_body_ps[:],
+                            hidden_bf[v][:, db, :],
+                            w2_signed[:, db, v, VIEWS:DIFFERENCES],
+                            start=(v == TITLE and db == 0),
+                            stop=(v == BODY and db == CB - 1),
+                        )
+                    nc.tensor.matmul(
+                        over_cat_ps[:],
+                        hidden_bf[v][:, db, :],
+                        w2_signed[:, db, v, 0:VIEWS],
+                        start=(v == TITLE and db == 0),
+                        stop=(v == CAT and db == CB - 1),
                     )
-                    queue.dma_start(out_blocks[:, cb, :], windows[cb][:])
+
+            def spread(column, name):
+                spread_ps = small_banks.tile([P, N], F32, name=name)
+                nc.tensor.transpose(spread_ps[:], column.to_broadcast([N, P]), identity[:])
+                return spread_ps
+
+            lean = held.tile([P, 1], F32, name="lean")
+            nc.scalar.activation(lean[:], title_over_body_ps[:], ACT.Tanh, scale=0.5)
+            lean_spread_ps = spread(lean[:], "lean_spread_ps")
+
+            grown = held.tile([P, VIEWS], F32, name="grown")
+            crowd = held.tile([P, 1], F32, name="crowd")
+            cat_weight = held.tile([P, 1], F32, name="cat_weight")
+            nc.scalar.activation(grown[:], over_cat_ps[:], ACT.Exp, accum_out=crowd[:])
+            nc.vector.reciprocal(cat_weight[:], crowd[:])
+            cat_weight_spread_ps = spread(cat_weight[:], "cat_weight_spread_ps")
+
+            tilt = held.tile([P, CB, N], F32, name="tilt")
+            minus_pair = held.tile([P, CB, N], F32, name="minus_pair")
+            first_two = held.tile([P, CB, N], F32, name="first_two")
+            scaled_cat = held.tile([P, CB, N], F32, name="scaled_cat")
+            for cb in range(CB):
+                nc.vector.scalar_tensor_tensor(tilt[:, cb, :], apart[:, cb, :], 0.5, lean_spread_ps[:], ALU.mult, ALU.mult)
+            for cb in range(CB):
+                nc.vector.scalar_tensor_tensor(minus_pair[:, cb, :], both[:, cb, :], -0.5, tilt[:, cb, :], ALU.mult, ALU.subtract)
+            for cb in range(CB):
+                nc.vector.tensor_tensor(scaled_cat[:, cb, :], view_sb[CAT][:, cb, :], cat_weight_spread_ps[:], ALU.mult)
+                nc.vector.scalar_tensor_tensor(
+                    first_two[:, cb, :], cat_weight_spread_ps[:], 1.0, minus_pair[:, cb, :], ALU.subtract, ALU.mult
+                )
+
+            for cb, queue in enumerate((nc.sync, nc.scalar)):
+                nc.vector.tensor_tensor(
+                    windows[cb][:].indirect(offsets[:]), first_two[:, cb, :], scaled_cat[:, cb, :], ALU.add
+                )
+                queue.dma_start(out_blocks[:, cb, :], windows[cb][:])

@@ -88,9 +88,7 @@ def tile_naml_kernel(tc, base, title, body, cat, w1, b1, w2, offs, out):
                     if SIGNS[v][difference] != 0.0:
                         nc.vector.tensor_scalar_mul(w2_signed[:, :, v, difference], w2_sb[:], SIGNS[v][difference])
 
-            both = held.tile([P, CB, N], F32, name="both")
             apart = held.tile([P, CB, N], F32, name="apart")
-            nc.vector.tensor_tensor(both[:], view_sb[TITLE][:], view_sb[BODY][:], ALU.add)
             nc.vector.tensor_tensor(apart[:], view_sb[TITLE][:], view_sb[BODY][:], ALU.subtract)
 
             for v in range(VIEWS):
@@ -132,9 +130,11 @@ def tile_naml_kernel(tc, base, title, body, cat, w1, b1, w2, offs, out):
             first_two = held.tile([P, CB, N], F32, name="first_two")
             scaled_cat = held.tile([P, CB, N], F32, name="scaled_cat")
             for cb in range(CB):
-                nc.vector.scalar_tensor_tensor(tilt[:, cb, :], apart[:, cb, :], 0.5, lean_spread_ps[:], ALU.mult, ALU.mult)
+                nc.vector.scalar_tensor_tensor(tilt[:, cb, :], lean_spread_ps[:], 1.0, apart[:, cb, :], ALU.add, ALU.mult)
             for cb in range(CB):
-                nc.vector.scalar_tensor_tensor(minus_pair[:, cb, :], both[:, cb, :], -0.5, tilt[:, cb, :], ALU.mult, ALU.subtract)
+                nc.vector.scalar_tensor_tensor(
+                    minus_pair[:, cb, :], tilt[:, cb, :], -0.5, view_sb[BODY][:, cb, :], ALU.mult, ALU.subtract
+                )
             for cb in range(CB):
                 nc.vector.tensor_tensor(scaled_cat[:, cb, :], view_sb[CAT][:, cb, :], cat_weight_spread_ps[:], ALU.mult)
                 nc.vector.scalar_tensor_tensor(

@@ -62,7 +62,7 @@ def tile_naml_kernel(tc, base, title, body, cat, w1, b1, w2, offs, out):
             tc.psum_pool(name="small_banks", bufs=1) as small_banks,
             tc.psum_pool(name="hidden_banks", bufs=2) as hidden_banks,
         ):
-            title_over_body_ps = small_banks.tile([P, 1], F32, name="title_over_body_ps")
+            title_over_body_ps = small_banks.tile([P, N], F32, name="title_over_body_ps")
             over_cat_ps = small_banks.tile([P, VIEWS], F32, name="over_cat_ps")
 
             for v in range(VIEWS):
@@ -89,15 +89,17 @@ def tile_naml_kernel(tc, base, title, body, cat, w1, b1, w2, offs, out):
                         nc.vector.tensor_scalar_mul(w2_signed[:, :, v, difference], w2_sb[:], SIGNS[v][difference])
 
             apart = held.tile([P, CB, N], F32, name="apart")
+            beyond = held.tile([P, CB, N], F32, name="beyond")
             nc.vector.tensor_tensor(apart[:], view_sb[TITLE][:], view_sb[BODY][:], ALU.subtract)
+            nc.vector.tensor_tensor(beyond[:], view_sb[CAT][:], view_sb[BODY][:], ALU.subtract)
 
             for v in range(VIEWS):
                 for db in range(CB):
                     if v != CAT:
                         nc.tensor.matmul(
                             title_over_body_ps[:],
+                            w2_signed[:, db, v, VIEWS:DIFFERENCES].to_broadcast([P, P]),
                             hidden_bf[v][:, db, :],
-                            w2_signed[:, db, v, VIEWS:DIFFERENCES],
                             start=(v == TITLE and db == 0),
                             stop=(v == BODY and db == CB - 1),
                         )
@@ -109,40 +111,34 @@ def tile_naml_kernel(tc, base, title, body, cat, w1, b1, w2, offs, out):
                         stop=(v == CAT and db == CB - 1),
                     )
 
-            def spread(column, name):
-                spread_ps = small_banks.tile([P, N], F32, name=name)
-                nc.tensor.transpose(spread_ps[:], column.to_broadcast([N, P]), identity[:])
-                return spread_ps
-
-            lean = held.tile([P, 1], F32, name="lean")
+            lean = held.tile([P, N], F32, name="lean")
             nc.scalar.activation(lean[:], title_over_body_ps[:], ACT.Tanh, scale=0.5)
-            lean_spread_ps = spread(lean[:], "lean_spread_ps")
 
             grown = held.tile([P, VIEWS], F32, name="grown")
             crowd = held.tile([P, 1], F32, name="crowd")
             cat_weight = held.tile([P, 1], F32, name="cat_weight")
             nc.scalar.activation(grown[:], over_cat_ps[:], ACT.Exp, accum_out=crowd[:])
             nc.vector.reciprocal(cat_weight[:], crowd[:])
-            cat_weight_spread_ps = spread(cat_weight[:], "cat_weight_spread_ps")
+            cat_weight_spread_ps = small_banks.tile([P, N], F32, name="cat_weight_spread_ps")
+            nc.tensor.transpose(cat_weight_spread_ps[:], cat_weight[:].to_broadcast([N, P]), identity[:])
 
             tilt = held.tile([P, CB, N], F32, name="tilt")
-            minus_pair = held.tile([P, CB, N], F32, name="minus_pair")
-            first_two = held.tile([P, CB, N], F32, name="first_two")
-            scaled_cat = held.tile([P, CB, N], F32, name="scaled_cat")
+            pair = held.tile([P, CB, N], F32, name="pair")
+            gap = held.tile([P, CB, N], F32, name="gap")
+            cat_part = held.tile([P, CB, N], F32, name="cat_part")
             for cb in range(CB):
-                nc.vector.scalar_tensor_tensor(tilt[:, cb, :], lean_spread_ps[:], 1.0, apart[:, cb, :], ALU.add, ALU.mult)
+                nc.vector.scalar_tensor_tensor(tilt[:, cb, :], lean[:], 1.0, apart[:, cb, :], ALU.add, ALU.mult)
+            for cb in range(CB):
+                nc.vector.scalar_tensor_tensor(gap[:, cb, :], tilt[:, cb, :], -0.5, beyond[:, cb, :], ALU.mult, ALU.add)
             for cb in range(CB):
                 nc.vector.scalar_tensor_tensor(
-                    minus_pair[:, cb, :], tilt[:, cb, :], -0.5, view_sb[BODY][:, cb, :], ALU.mult, ALU.subtract
+                    pair[:, cb, :], tilt[:, cb, :], 0.5, view_sb[BODY][:, cb, :], ALU.mult, ALU.add
                 )
             for cb in range(CB):
-                nc.vector.tensor_tensor(scaled_cat[:, cb, :], view_sb[CAT][:, cb, :], cat_weight_spread_ps[:], ALU.mult)
-                nc.vector.scalar_tensor_tensor(
-                    first_two[:, cb, :], cat_weight_spread_ps[:], 1.0, minus_pair[:, cb, :], ALU.subtract, ALU.mult
-                )
+                nc.vector.tensor_tensor(cat_part[:, cb, :], gap[:, cb, :], cat_weight_spread_ps[:], ALU.mult)
 
             for cb, queue in enumerate((nc.sync, nc.scalar)):
                 nc.vector.tensor_tensor(
-                    windows[cb][:].indirect(offsets[:]), first_two[:, cb, :], scaled_cat[:, cb, :], ALU.add
+                    windows[cb][:].indirect(offsets[:]), pair[:, cb, :], cat_part[:, cb, :], ALU.add
                 )
                 queue.dma_start(out_blocks[:, cb, :], windows[cb][:])

@@ -28,11 +28,15 @@ def tile_naml_kernel(tc, base, title, body, cat, w1, b1, w2, offs, out):
         view_sb = [held.tile([P, CB, N], F32, name=f"view_sb{v}") for v in range(VIEWS)]
         offsets = held.tile([P, N // 16], U16, name="offsets")
         nc.scalar.dma_start(w1_sb[:], w1.rearrange("(p kb) d -> p kb d", p=P))
-        for v, (view, queue) in enumerate(((title, nc.sync), (body, nc.scalar), (cat, nc.sync))):
+
+        def load_view(v, view, queue):
             queue.dma_start(view_sb[v][:], view.rearrange("(p cb) j -> p cb j", p=P))
-        with nc.allow_non_contiguous_dma(reason="one element to a partition: 256 small pieces, once"):
-            nc.sync.dma_start(b1_sb[:], b1.rearrange("(db p) o -> p (db o)", p=P))
-            nc.scalar.dma_start(w2_sb[:], w2.rearrange("(db p) o -> p (db o)", p=P))
+
+        load_view(TITLE, title, nc.sync)
+        nc.sync.dma_start(b1_sb[:], b1.rearrange("(p db) o -> p (db o)", p=P))
+        load_view(BODY, body, nc.scalar)
+        load_view(CAT, cat, nc.sync)
+        nc.scalar.dma_start(w2_sb[:], w2.rearrange("(p db) o -> p (db o)", p=P))
         nc.sync.dma_start(offsets[:], offs)
         base_blocks = base.rearrange("(p cb) s -> p cb s", p=P)
         out_blocks = out.rearrange("(p cb) s -> p cb s", p=P)
@@ -73,7 +77,7 @@ def tile_naml_kernel(tc, base, title, body, cat, w1, b1, w2, offs, out):
                     for db in range(CB):
                         nc.tensor.matmul(
                             hidden_ps[db][:],
-                            w1_sb[:, kb, db * P : (db + 1) * P],
+                            w1_sb[:, kb, db::CB],
                             view_bf[:, kb, :],
                             start=(kb == 0),
                             stop=(kb == CB - 1),

import concourse.mybir as mybir
from concourse.masks import make_identity

P = 128
C, S, N = 256, 256, 128
CB = C // P
VIEWS = 3
TITLE, BODY, CAT = 0, 1, 2
F32, BF16, U16 = mybir.dt.float32, mybir.dt.bfloat16, mybir.dt.uint16
ALU = mybir.AluOpType
ACT = mybir.ActivationFunctionType

SIGNS = ((1.0, 0.0, 0.0, 1.0), (0.0, 1.0, 0.0, -1.0), (-1.0, -1.0, 0.0, 0.0))
DIFFERENCES = VIEWS + 1

WARM_COLUMNS = 512
WARM_TURNS = 4

FLOPS = 2 * C * C * VIEWS * N + 2 * C * VIEWS * N


def tile_naml_kernel(tc, base, title, body, cat, w1, b1, w2, offs, out):
    nc = tc.nc
    with tc.tile_pool(name="held", bufs=1) as held:
        b1_sb = held.tile([P, CB], F32, name="b1_sb")
        w2_sb = held.tile([P, CB], BF16, name="w2_sb")
        w1_sb = held.tile([P, CB, C], BF16, name="w1_sb")
        view_sb = [held.tile([P, CB, N], F32, name=f"view_sb{v}") for v in range(VIEWS)]
        offsets = held.tile([P, N // 16], U16, name="offsets")
        nc.scalar.dma_start(w1_sb[:], w1.rearrange("(p kb) d -> p kb d", p=P))

        def load_view(v, view, queue):
            queue.dma_start(view_sb[v][:], view.rearrange("(p cb) j -> p cb j", p=P))

        load_view(TITLE, title, nc.sync)
        nc.sync.dma_start(b1_sb[:], b1.rearrange("(p db) o -> p (db o)", p=P))
        load_view(BODY, body, nc.scalar)
        load_view(CAT, cat, nc.sync)
        nc.scalar.dma_start(w2_sb[:], w2.rearrange("(p db) o -> p (db o)", p=P))
        nc.sync.dma_start(offsets[:], offs)
        base_blocks = base.rearrange("(p cb) s -> p cb s", p=P)
        out_blocks = out.rearrange("(p cb) s -> p cb s", p=P)
        windows = []
        for cb in range(CB):
            window = held.tile([P, S], F32, name=f"window{cb}")
            nc.sync.dma_start(window[:], base_blocks[:, cb, :])
            windows.append(window)

        zero = held.tile([P, 1], BF16, name="zero")
        nc.gpsimd.memset(zero[:], 0.0)
        with tc.psum_pool(name="warm_bank", bufs=1) as warm_bank:
            warm_ps = warm_bank.tile([P, WARM_COLUMNS], F32, name="warm_ps")
            for turn in range(WARM_TURNS):
                nc.tensor.matmul(
                    warm_ps[:], zero[:].to_broadcast([P, P]), zero[:].to_broadcast([P, WARM_COLUMNS]), start=True, stop=True
                )

        scratch = held.tile([P, 1], F32, name="scratch")
        nc.vector.memset(scratch[:], 0.0)
        nc.scalar.activation(scratch[:], scratch[:], ACT.Tanh)
        identity = held.tile([P, P], F32, name="identity")
        make_identity(nc, identity[:])

        hidden_bf = [held.tile([P, CB, N], BF16, name=f"hidden_bf{v}") for v in range(VIEWS)]
        with (
            tc.psum_pool(name="small_banks", bufs=1) as small_banks,
            tc.psum_pool(name="hidden_banks", bufs=2) as hidden_banks,
        ):
            title_over_body_ps = small_banks.tile([P, N], F32, name="title_over_body_ps")
            over_cat_ps = small_banks.tile([P, VIEWS], F32, name="over_cat_ps")

            for v in range(VIEWS):
                view_bf = held.tile([P, CB, N], BF16, name=f"view_bf{v}")
                hidden_ps = [hidden_banks.tile([P, N], F32, name=f"hidden_ps{db}") for db in range(CB)]
                for kb in range(CB):
                    nc.vector.tensor_copy(view_bf[:, kb, :], view_sb[v][:, kb, :])
                    for db in range(CB):
                        nc.tensor.matmul(
                            hidden_ps[db][:],
                            w1_sb[:, kb, db::CB],
                            view_bf[:, kb, :],
                            start=(kb == 0),
                            stop=(kb == CB - 1),
                        )
                for db in range(CB):
                    nc.scalar.activation(hidden_bf[v][:, db, :], hidden_ps[db][:], ACT.Tanh, bias=b1_sb[:, db : db + 1])

            w2_signed = held.tile([P, CB, VIEWS, DIFFERENCES], BF16, name="w2_signed")
            nc.vector.memset(w2_signed[:], 0.0)
            for v in range(VIEWS):
                for difference in range(DIFFERENCES):
                    if SIGNS[v][difference] != 0.0:
                        nc.vector.tensor_scalar_mul(w2_signed[:, :, v, difference], w2_sb[:], SIGNS[v][difference])

            apart = held.tile([P, CB, N], F32, name="apart")
            beyond = held.tile([P, CB, N], F32, name="beyond")
            nc.vector.tensor_tensor(apart[:], view_sb[TITLE][:], view_sb[BODY][:], ALU.subtract)
            nc.vector.tensor_tensor(beyond[:], view_sb[CAT][:], view_sb[BODY][:], ALU.subtract)

            for v in range(VIEWS):
                for db in range(CB):
                    if v != CAT:
                        nc.tensor.matmul(
                            title_over_body_ps[:],
                            w2_signed[:, db, v, VIEWS:DIFFERENCES].to_broadcast([P, P]),
                            hidden_bf[v][:, db, :],
                            start=(v == TITLE and db == 0),
                            stop=(v == BODY and db == CB - 1),
                        )
                    nc.tensor.matmul(
                        over_cat_ps[:],
                        hidden_bf[v][:, db, :],
                        w2_signed[:, db, v, 0:VIEWS],
                        start=(v == TITLE and db == 0),
                        stop=(v == CAT and db == CB - 1),
                    )

            lean = held.tile([P, N], F32, name="lean")
            nc.scalar.activation(lean[:], title_over_body_ps[:], ACT.Tanh, scale=0.5)

            grown = held.tile([P, VIEWS], F32, name="grown")
            crowd = held.tile([P, 1], F32, name="crowd")
            cat_weight = held.tile([P, 1], F32, name="cat_weight")
            nc.scalar.activation(grown[:], over_cat_ps[:], ACT.Exp, accum_out=crowd[:])
            nc.vector.reciprocal(cat_weight[:], crowd[:])
            cat_weight_spread_ps = small_banks.tile([P, N], F32, name="cat_weight_spread_ps")
            nc.tensor.transpose(cat_weight_spread_ps[:], cat_weight[:].to_broadcast([N, P]), identity[:])

            tilt = held.tile([P, CB, N], F32, name="tilt")
            pair = held.tile([P, CB, N], F32, name="pair")
            gap = held.tile([P, CB, N], F32, name="gap")
            cat_part = held.tile([P, CB, N], F32, name="cat_part")
            for cb in range(CB):
                nc.vector.scalar_tensor_tensor(tilt[:, cb, :], lean[:], 1.0, apart[:, cb, :], ALU.add, ALU.mult)
            for cb in range(CB):
                nc.vector.scalar_tensor_tensor(gap[:, cb, :], tilt[:, cb, :], -0.5, beyond[:, cb, :], ALU.mult, ALU.add)
            for cb in range(CB):
                nc.vector.scalar_tensor_tensor(
                    pair[:, cb, :], tilt[:, cb, :], 0.5, view_sb[BODY][:, cb, :], ALU.mult, ALU.add
                )
            for cb in range(CB):
                nc.vector.tensor_tensor(cat_part[:, cb, :], gap[:, cb, :], cat_weight_spread_ps[:], ALU.mult)

            for cb, queue in enumerate((nc.sync, nc.scalar)):
                nc.vector.tensor_tensor(
                    windows[cb][:].indirect(offsets[:]), pair[:, cb, :], cat_part[:, cb, :], ALU.add
                )
                queue.dma_start(out_blocks[:, cb, :], windows[cb][:])
